import numpy as np
import ml_dtypes


def mxq(x, axis, fmt="e4m3"):
    dtype, down = {"e4m3": (ml_dtypes.float8_e4m3fn, 7), "e5m2": (ml_dtypes.float8_e5m2, 14)}[fmt]
    v = np.moveaxis(np.asarray(x, np.float32).astype(ml_dtypes.bfloat16).astype(np.float64), axis, -1)
    blocks = v.reshape(v.shape[:-1] + (-1, 32))
    amax = np.abs(blocks).max(-1, keepdims=True)
    byte = np.maximum(np.where(amax > 0, np.frexp(amax)[1] - 1 + 127, 0) - down, 1)
    scale = np.exp2(byte - 127.0)
    codes = (blocks / scale).astype(np.float32).astype(dtype).astype(np.float64)
    return np.moveaxis((codes * scale).reshape(v.shape), -1, axis)


WIDE = False


def mx_kscale(k):
    if not WIDE:
        return np.ones(k)
    levels = np.array([10, -10, 5, -5, 0])
    a = np.random.permutation(np.resize(levels, k // 512 * 4)).reshape(k // 512, 4)
    idx = np.arange(k)
    return np.exp2(a[idx // 512, idx % 128 // 32])


BF16 = ml_dtypes.bfloat16


def bf(x):
    return np.asarray(x, np.float32).astype(BF16)


def f64(x):
    return np.asarray(x).astype(np.float64)


E2M1 = np.array([0.0, 0.5, 1.0, 1.5, 2.0, 3.0, 4.0, 6.0, -0.0, -0.5, -1.0, -1.5, -2.0, -3.0, -4.0, -6.0])


def pack_weight(w, fmt):
    k, n = w.shape
    w = f64(bf(w)).reshape(k // 32, 32, n)
    amax = np.abs(w).max(1)
    if fmt == "e4m3":
        byte = np.frexp(amax)[1] - 1 + 127 - 7
    else:
        mant, ex = np.frexp(amax / 6.0)
        byte = np.where(mant > 0.5, ex, ex - 1) + 127
    byte = np.clip(np.where(amax > 0, byte, 1), 1, 254)
    scaled = (w * np.exp2(127.0 - byte)[:, None, :]).reshape(k, n).astype(np.float32)
    by_word = np.ascontiguousarray(scaled.reshape(k // 512, 128, 4, n).transpose(0, 1, 3, 2))
    if fmt == "e4m3":
        words = by_word.astype(ml_dtypes.float8_e4m3fn).view(np.uint8)
    else:
        c = by_word.astype(ml_dtypes.float4_e2m1fn).view(np.uint8) & 0xF
        words = c[..., 0::2] | (c[..., 1::2] << 4)
    return np.ascontiguousarray(words), np.ascontiguousarray(byte.astype(np.uint8).reshape(k // 512, 16, n))


def unpack_weight(words, scales, fmt):
    g, p, n, _ = words.shape
    if fmt == "e4m3":
        vals = np.ascontiguousarray(words).view(ml_dtypes.float8_e4m3fn).astype(np.float64)
    else:
        nib = np.empty((g, p, n, 4), np.uint8)
        nib[..., 0::2] = words & 0xF
        nib[..., 1::2] = words >> 4
        vals = E2M1[nib]
    vals = vals * np.repeat(np.exp2(scales.astype(np.float64) - 127.0), 8, axis=1)[..., None]
    return vals.transpose(0, 1, 3, 2).reshape(g * 512, n)


B, HI, WI, F, D, NH, C = 1, 32, 32, 1024, 256, 3, 16
N = HI * WI
EPS = 1e-12
FMT = "e4m3"


def l2norm_rows(a):
    n = np.sqrt(np.sum(a * a, axis=1, keepdims=True))
    return a / np.maximum(n, EPS)


def setup_inputs():
    s = mx_kscale(F)

    def w():
        full = np.random.standard_normal((D, F)) / np.sqrt(F) / s[None, :]
        return pack_weight(np.ascontiguousarray(full.T), FMT)

    def b():
        return bf(np.random.standard_normal(D) * 0.2)

    x = bf(np.random.standard_normal((B, F, HI, WI)) * s[None, :, None, None])
    W1_words, W1_scales = w()
    b1 = b()
    W2_words, W2_scales = w()
    b2 = b()
    W3_words, W3_scales = w()
    b3 = b()
    return {"x": x,
            "W1_words": W1_words, "W1_scales": W1_scales, "b1": b1,
            "W2_words": W2_words, "W2_scales": W2_scales, "b2": b2,
            "W3_words": W3_words, "W3_scales": W3_scales, "b3": b3}


def reference(x, W1_words, W1_scales, b1, W2_words, W2_scales, b2, W3_words, W3_scales, b3):
    xq = mxq(f64(x).reshape(F, N).T, 1, "e4m3")
    heads = [l2norm_rows((xq @ unpack_weight(words, scales, FMT)) + f64(b))
             for words, scales, b in ((W1_words, W1_scales, b1), (W2_words, W2_scales, b2), (W3_words, W3_scales, b3))]
    return np.stack(heads)

@@ -1,0 +1,180 @@
+from contextlib import ExitStack
+
+import concourse.mybir as mybir
+
+F32 = mybir.dt.float32
+BF16 = mybir.dt.bfloat16
+I32 = mybir.dt.int32
+U32 = mybir.dt.uint32
+U8 = mybir.dt.uint8
+FP8X4 = mybir.dt.float8_e4m3fn_x4
+ACT = mybir.ActivationFunctionType
+ALU = mybir.AluOpType
+
+P = 128
+PACK = 4
+K_PASS = P * PACK
+FEATURES = 1024
+NODES = 1024
+HEADS = 3
+HEAD_DIM = 256
+PASSES = FEATURES // K_PASS
+TILES = 2
+CHUNK = TILES * P
+CHUNKS = NODES // CHUNK
+QUADRANTS = 4
+RUN = 4
+EPS_SQUARED = 1e-24
+
+FLOPS = 2 * NODES * FEATURES * HEADS * HEAD_DIM
+
+
+def tile_gat_pa_kernel(
+    tc, x, W1_words, W1_scales, b1, W2_words, W2_scales, b2, W3_words, W3_scales, b3, out
+):
+    nc = tc.nc
+    weights = ((W1_words, W1_scales, b1), (W2_words, W2_scales, b2), (W3_words, W3_scales, b3))
+    x_rows = x.rearrange("b f i j -> (b f) (i j)").rearrange("(g p t) n -> g p t n", p=P, t=PACK)
+
+    with ExitStack() as ctx:
+        const = ctx.enter_context(tc.tile_pool(name="const", bufs=1))
+        raw_pool = ctx.enter_context(tc.tile_pool(name="raw", bufs=CHUNKS * PASSES))
+        grouped_pool = ctx.enter_context(tc.tile_pool(name="grouped", bufs=CHUNKS))
+        xq_pool = ctx.enter_context(tc.tile_pool(name="xq", bufs=CHUNKS))
+        rows_pool = ctx.enter_context(tc.tile_pool(name="rows", bufs=HEADS * CHUNKS))
+        small = ctx.enter_context(tc.tile_pool(name="small", bufs=4))
+        psum = ctx.enter_context(tc.psum_pool(name="psum", bufs=8))
+
+        w_codes = []
+        w_scales = []
+        bias_row = []
+        bias_all = []
+        for h in range(HEADS):
+            codes = const.tile([P, PASSES, HEAD_DIM], U32, name="w_codes%d" % h, align_bytes=64)
+            plane = const.tile([P, PASSES, HEAD_DIM], U8, name="w_scales%d" % h, align_bytes=64)
+            row = const.tile([P, HEAD_DIM], BF16, name="bias_row%d" % h)
+            spread = const.tile([P, HEAD_DIM], F32, name="bias_all%d" % h)
+            nc.vector.memset(plane[:].bitcast(I32), 0)
+            nc.vector.memset(row[:], 0.0)
+            w_codes.append(codes)
+            w_scales.append(plane)
+            bias_row.append(row)
+            bias_all.append(spread)
+        ones = const.tile([P, P], BF16, name="ones")
+        nc.vector.memset(ones[:], 1.0)
+
+        warm = const.tile([P, 1], F32, name="warm")
+        nc.vector.memset(warm[:], 1.0)
+        nc.scalar.activation(out=warm[:], in_=warm[:], func=ACT.Sqrt)
+
+        x_raw = {}
+
+        def load_x(u):
+            for g in range(PASSES):
+                raw = raw_pool.tile([P, PACK, CHUNK], BF16, name="raw")
+                nc.sync.dma_start(out=raw[:], in_=x_rows[g, :, :, u * CHUNK : (u + 1) * CHUNK])
+                x_raw[(u, g)] = raw
+
+        def load_weight(h):
+            words, scales, bias = weights[h]
+            for q in range(QUADRANTS):
+                nc.sync.dma_start(
+                    out=w_scales[h][32 * q : 32 * q + 4, :, :].bitcast(I32),
+                    in_=scales[:, 4 * q : 4 * q + 4, :].rearrange("g r n -> r g n").bitcast(I32),
+                )
+            nc.sync.dma_start(
+                out=w_codes[h][:].bitcast(I32),
+                in_=words.rearrange("g p n t -> p g (n t)").bitcast(I32),
+            )
+            nc.gpsimd.dma_start(out=bias_row[h][0:1, :], in_=bias.unsqueeze(0))
+
+        load_x(0)
+        load_weight(0)
+        for u in range(1, CHUNKS):
+            load_x(u)
+        for h in range(1, HEADS):
+            load_weight(h)
+
+        x_codes = {}
+        x_scales = {}
+
+        def quantise(u):
+            grouped = grouped_pool.tile([P, PASSES, CHUNK, PACK], BF16, name="grouped", align_bytes=64)
+            nc.vector.tensor_copy(
+                out=grouped[:, 0, :, :].rearrange("p (c i) t -> p c t i", i=RUN),
+                in_=x_raw[(u, 0)][:].rearrange("p t (c i) -> p c t i", i=RUN),
+            )
+            nc.scalar.copy(
+                out=grouped[:, 1, :, :].rearrange("p (c i) t -> p c t i", i=RUN),
+                in_=x_raw[(u, 1)][:].rearrange("p t (c i) -> p c t i", i=RUN),
+            )
+            codes = xq_pool.tile([P, PASSES * CHUNK], U32, name="x_codes", align_bytes=64)
+            plane = xq_pool.tile([P, PASSES * CHUNK], U8, name="x_scales", align_bytes=64)
+            nc.vector.quantize_mx(
+                out=codes[:].bitcast(FP8X4),
+                scales=plane[:],
+                in_=grouped[:].rearrange("p g n t -> p (g n t)"),
+            )
+            x_codes[u] = codes
+            x_scales[u] = plane
+
+        def spread_bias(h):
+            bank = psum.tile([P, TILES, HEAD_DIM], F32, name="acc")
+            nc.tensor.matmul(out=bank[:, 0, :], lhsT=ones[:], rhs=bias_row[h][:], start=True, stop=True)
+            nc.scalar.copy(out=bias_all[h][:], in_=bank[:, 0, :])
+
+        def project(h, u):
+            acc = psum.tile([P, TILES, HEAD_DIM], F32, name="acc")
+            for i in range(TILES):
+                for g in range(PASSES):
+                    nodes = slice(g * CHUNK + i * P, g * CHUNK + (i + 1) * P)
+                    nc.tensor.matmul_mx(
+                        out=acc[:, i, :],
+                        lhsT=x_codes[u][:, nodes].bitcast(FP8X4),
+                        lhsT_scale=x_scales[u][:, nodes],
+                        rhs=w_codes[h][:, g, :].bitcast(FP8X4),
+                        rhs_scale=w_scales[h][:, g, :],
+                        start=(g == 0),
+                        stop=(g == PASSES - 1),
+                    )
+            return acc
+
+        def normalise(h, u, acc):
+            rows = rows_pool.tile([P, TILES, HEAD_DIM], F32, name="rows")
+            nc.vector.tensor_tensor(
+                out=rows[:],
+                in0=acc[:],
+                in1=bias_all[h][:].unsqueeze(1).to_broadcast([P, TILES, HEAD_DIM]),
+                op=ALU.add,
+            )
+            sum_sq = small.tile([P, TILES], F32, name="sum_sq")
+            for i in range(TILES):
+                squares = small.tile([P, HEAD_DIM], F32, name="squares")
+                nc.scalar.activation(
+                    out=squares[:], in_=rows[:, i, :], func=ACT.Square, accum_out=sum_sq[:, i : i + 1]
+                )
+            excess = small.tile([P, TILES], F32, name="excess")
+            nc.scalar.activation(out=excess[:], in_=sum_sq[:], func=ACT.Relu, bias=-EPS_SQUARED)
+            norm = small.tile([P, TILES], F32, name="norm")
+            nc.scalar.activation(out=norm[:], in_=excess[:], func=ACT.Sqrt, bias=EPS_SQUARED)
+            inverse = small.tile([P, TILES], F32, name="inverse")
+            nc.vector.reciprocal(out=inverse[:], in_=norm[:])
+            for i in range(TILES):
+                nc.vector.tensor_scalar(
+                    out=rows[:, i, :],
+                    in0=rows[:, i, :],
+                    scalar1=inverse[:, i : i + 1],
+                    scalar2=None,
+                    op0=ALU.mult,
+                )
+            nc.sync.dma_start(
+                out=out[h, u * CHUNK : (u + 1) * CHUNK, :].rearrange("(i p) d -> p i d", p=P),
+                in_=rows[:],
+            )
+
+        for h in range(HEADS):
+            spread_bias(h)
+            for u in range(CHUNKS):
+                if h == 0:
+                    quantise(u)
+                normalise(h, u, project(h, u))

@@ -22,9 +22,14 @@ PASSES = FEATURES // K_PASS
 TILES = 2
 CHUNK = TILES * P
 CHUNKS = NODES // CHUNK
+UNITS = HEADS * CHUNKS
+LOAD = 2 * CHUNK
+LOADS = NODES // LOAD
 QUADRANTS = 4
 RUN = 4
 EPS_SQUARED = 1e-24
+AHEAD = 2
+LAG = 2
 
 FLOPS = 2 * NODES * FEATURES * HEADS * HEAD_DIM
 
@@ -37,46 +42,48 @@ def tile_gat_pa_kernel(
     x_rows = x.rearrange("b f i j -> (b f) (i j)").rearrange("(g p t) n -> g p t n", p=P, t=PACK)
 
     with ExitStack() as ctx:
+        ctx.enter_context(tc.manual_schedule())
         const = ctx.enter_context(tc.tile_pool(name="const", bufs=1))
-        raw_pool = ctx.enter_context(tc.tile_pool(name="raw", bufs=CHUNKS * PASSES))
+        raw_pool = ctx.enter_context(tc.tile_pool(name="raw", bufs=LOADS * PASSES))
         grouped_pool = ctx.enter_context(tc.tile_pool(name="grouped", bufs=CHUNKS))
         xq_pool = ctx.enter_context(tc.tile_pool(name="xq", bufs=CHUNKS))
-        rows_pool = ctx.enter_context(tc.tile_pool(name="rows", bufs=HEADS * CHUNKS))
-        small = ctx.enter_context(tc.tile_pool(name="small", bufs=4))
+        rows_pool = ctx.enter_context(tc.tile_pool(name="rows", bufs=UNITS))
+        small = ctx.enter_context(tc.tile_pool(name="small", bufs=LAG + 3))
         psum = ctx.enter_context(tc.psum_pool(name="psum", bufs=8))
 
         w_codes = []
         w_scales = []
         bias_row = []
-        bias_all = []
+        bias_all = {}
+        for h in range(HEADS):
+            row = const.tile([P, HEAD_DIM], BF16, name="bias_row%d" % h)
+            nc.vector.memset(row[:], 0.0)
+            bias_row.append(row)
         for h in range(HEADS):
             codes = const.tile([P, PASSES, HEAD_DIM], U32, name="w_codes%d" % h, align_bytes=64)
             plane = const.tile([P, PASSES, HEAD_DIM], U8, name="w_scales%d" % h, align_bytes=64)
-            row = const.tile([P, HEAD_DIM], BF16, name="bias_row%d" % h)
-            spread = const.tile([P, HEAD_DIM], F32, name="bias_all%d" % h)
             nc.vector.memset(plane[:].bitcast(I32), 0)
-            nc.vector.memset(row[:], 0.0)
             w_codes.append(codes)
             w_scales.append(plane)
-            bias_row.append(row)
-            bias_all.append(spread)
         ones = const.tile([P, P], BF16, name="ones")
         nc.vector.memset(ones[:], 1.0)
-
         warm = const.tile([P, 1], F32, name="warm")
         nc.vector.memset(warm[:], 1.0)
-        nc.scalar.activation(out=warm[:], in_=warm[:], func=ACT.Sqrt)
+
+        nc.scalar.activation(out=warm[:], in_=warm[:], func=ACT.Abs_reciprocal_sqrt)
 
         x_raw = {}
 
-        def load_x(u):
+        def load_x(v):
             for g in range(PASSES):
-                raw = raw_pool.tile([P, PACK, CHUNK], BF16, name="raw")
-                nc.sync.dma_start(out=raw[:], in_=x_rows[g, :, :, u * CHUNK : (u + 1) * CHUNK])
-                x_raw[(u, g)] = raw
+                raw = raw_pool.tile([P, PACK, LOAD], BF16, name="raw")
+                nc.sync.dma_start(out=raw[:], in_=x_rows[g, :, :, v * LOAD : (v + 1) * LOAD])
+                for u in range(v * LOAD // CHUNK, (v + 1) * LOAD // CHUNK):
+                    x_raw[(u, g)] = raw[:, :, u * CHUNK - v * LOAD : (u + 1) * CHUNK - v * LOAD]
 
         def load_weight(h):
             words, scales, bias = weights[h]
+            nc.sync.dma_start(out=bias_row[h][0:1, :], in_=bias.unsqueeze(0))
             for q in range(QUADRANTS):
                 nc.sync.dma_start(
                     out=w_scales[h][32 * q : 32 * q + 4, :, :].bitcast(I32),
@@ -86,44 +93,61 @@ def tile_gat_pa_kernel(
                 out=w_codes[h][:].bitcast(I32),
                 in_=words.rearrange("g p n t -> p g (n t)").bitcast(I32),
             )
-            nc.gpsimd.dma_start(out=bias_row[h][0:1, :], in_=bias.unsqueeze(0))
 
         load_x(0)
         load_weight(0)
-        for u in range(1, CHUNKS):
-            load_x(u)
+        for v in range(1, LOADS):
+            load_x(v)
         for h in range(1, HEADS):
             load_weight(h)
 
+        def spread_bias(h):
+            bank = psum.tile([P, TILES, HEAD_DIM], F32, name="acc")
+            nc.tensor.matmul(out=bank[:, 0, :], lhsT=ones[:], rhs=bias_row[h][:], start=True, stop=True)
+            spread = const.tile([P, HEAD_DIM], F32, name="bias_all%d" % h)
+            nc.scalar.copy(out=spread[:], in_=bank[:, 0, :])
+            bias_all[h] = spread
+
+        x_grouped = {}
         x_codes = {}
         x_scales = {}
 
-        def quantise(u):
+        def regroup(u):
             grouped = grouped_pool.tile([P, PASSES, CHUNK, PACK], BF16, name="grouped", align_bytes=64)
-            nc.vector.tensor_copy(
-                out=grouped[:, 0, :, :].rearrange("p (c i) t -> p c t i", i=RUN),
-                in_=x_raw[(u, 0)][:].rearrange("p t (c i) -> p c t i", i=RUN),
-            )
-            nc.scalar.copy(
-                out=grouped[:, 1, :, :].rearrange("p (c i) t -> p c t i", i=RUN),
-                in_=x_raw[(u, 1)][:].rearrange("p t (c i) -> p c t i", i=RUN),
-            )
+            for g in range(PASSES):
+                nc.vector.tensor_copy(
+                    out=grouped[:, g, 0:P, :].rearrange("p (c i) t -> p c t i", i=RUN),
+                    in_=x_raw[(u, g)][:, :, 0:P].rearrange("p t (c i) -> p c t i", i=RUN),
+                )
+                nc.scalar.copy(
+                    out=grouped[:, g, P:CHUNK, :].rearrange("p (c i) t -> p c t i", i=RUN),
+                    in_=x_raw[(u, g)][:, :, P:CHUNK].rearrange("p t (c i) -> p c t i", i=RUN),
+                )
+            x_grouped[u] = grouped
+
+        def quantise(u):
             codes = xq_pool.tile([P, PASSES * CHUNK], U32, name="x_codes", align_bytes=64)
             plane = xq_pool.tile([P, PASSES * CHUNK], U8, name="x_scales", align_bytes=64)
             nc.vector.quantize_mx(
                 out=codes[:].bitcast(FP8X4),
                 scales=plane[:],
-                in_=grouped[:].rearrange("p g n t -> p (g n t)"),
+                in_=x_grouped[u][:].rearrange("p g n t -> p (g n t)"),
             )
             x_codes[u] = codes
             x_scales[u] = plane
 
-        def spread_bias(h):
-            bank = psum.tile([P, TILES, HEAD_DIM], F32, name="acc")
-            nc.tensor.matmul(out=bank[:, 0, :], lhsT=ones[:], rhs=bias_row[h][:], start=True, stop=True)
-            nc.scalar.copy(out=bias_all[h][:], in_=bank[:, 0, :])
+        acc_of = {}
+        rows_of = {}
+        inverse_of = {}
 
-        def project(h, u):
+        def prepare(k):
+            h, u = divmod(k, CHUNKS)
+            if u == 0:
+                spread_bias(h)
+            if h == 0:
+                quantise(u)
+                if u + 1 < CHUNKS:
+                    regroup(u + 1)
             acc = psum.tile([P, TILES, HEAD_DIM], F32, name="acc")
             for i in range(TILES):
                 for g in range(PASSES):
@@ -137,33 +161,50 @@ def tile_gat_pa_kernel(
                         start=(g == 0),
                         stop=(g == PASSES - 1),
                     )
-            return acc
+            acc_of[k] = acc
 
-        def normalise(h, u, acc):
+        sum_sq_of = {}
+        excess_of = {}
+
+        def add_bias(k):
+            h = k // CHUNKS
             rows = rows_pool.tile([P, TILES, HEAD_DIM], F32, name="rows")
             nc.vector.tensor_tensor(
                 out=rows[:],
-                in0=acc[:],
+                in0=acc_of[k][:],
                 in1=bias_all[h][:].unsqueeze(1).to_broadcast([P, TILES, HEAD_DIM]),
                 op=ALU.add,
             )
+            rows_of[k] = rows
             sum_sq = small.tile([P, TILES], F32, name="sum_sq")
-            for i in range(TILES):
-                squares = small.tile([P, HEAD_DIM], F32, name="squares")
-                nc.scalar.activation(
-                    out=squares[:], in_=rows[:, i, :], func=ACT.Square, accum_out=sum_sq[:, i : i + 1]
-                )
+            sum_sq_of[k] = sum_sq
+
+        def sum_squares(k, i):
+            squares = small.tile([P, HEAD_DIM], F32, name="squares")
+            nc.scalar.activation(
+                out=squares[:], in_=rows_of[k][:, i, :], func=ACT.Square, accum_out=sum_sq_of[k][:, i : i + 1]
+            )
+
+        def clamp(k):
             excess = small.tile([P, TILES], F32, name="excess")
-            nc.scalar.activation(out=excess[:], in_=sum_sq[:], func=ACT.Relu, bias=-EPS_SQUARED)
-            norm = small.tile([P, TILES], F32, name="norm")
-            nc.scalar.activation(out=norm[:], in_=excess[:], func=ACT.Sqrt, bias=EPS_SQUARED)
+            nc.scalar.activation(out=excess[:], in_=sum_sq_of[k][:], func=ACT.Relu, bias=-EPS_SQUARED)
+            excess_of[k] = excess
+
+        def invert(k):
             inverse = small.tile([P, TILES], F32, name="inverse")
-            nc.vector.reciprocal(out=inverse[:], in_=norm[:])
+            nc.scalar.activation(
+                out=inverse[:], in_=excess_of[k][:], func=ACT.Abs_reciprocal_sqrt, bias=EPS_SQUARED
+            )
+            inverse_of[k] = inverse
+
+        def scale_and_store(k):
+            h, u = divmod(k, CHUNKS)
+            rows = rows_of[k]
             for i in range(TILES):
                 nc.vector.tensor_scalar(
                     out=rows[:, i, :],
                     in0=rows[:, i, :],
-                    scalar1=inverse[:, i : i + 1],
+                    scalar1=inverse_of[k][:, i : i + 1],
                     scalar2=None,
                     op0=ALU.mult,
                 )
@@ -172,9 +213,21 @@ def tile_gat_pa_kernel(
                 in_=rows[:],
             )
 
-        for h in range(HEADS):
-            spread_bias(h)
-            for u in range(CHUNKS):
-                if h == 0:
-                    quantise(u)
-                normalise(h, u, project(h, u))
+        regroup(0)
+        for k in range(AHEAD):
+            prepare(k)
+        for k in range(UNITS + LAG):
+            if k < UNITS:
+                add_bias(k)
+            if k < UNITS:
+                sum_squares(k, 0)
+            if 1 <= k <= UNITS:
+                clamp(k - 1)
+            if k < UNITS:
+                sum_squares(k, 1)
+            if 1 <= k <= UNITS:
+                invert(k - 1)
+            if k + AHEAD < UNITS:
+                prepare(k + AHEAD)
+            if k >= LAG:
+                scale_and_store(k - LAG)

@@ -23,13 +23,11 @@ TILES = 2
 CHUNK = TILES * P
 CHUNKS = NODES // CHUNK
 UNITS = HEADS * CHUNKS
-LOAD = 2 * CHUNK
-LOADS = NODES // LOAD
 QUADRANTS = 4
 RUN = 4
-EPS_SQUARED = 1e-24
+EPS = 1e-12
 AHEAD = 2
-LAG = 2
+LAG = 3
 
 FLOPS = 2 * NODES * FEATURES * HEADS * HEAD_DIM
 
@@ -44,7 +42,7 @@ def tile_gat_pa_kernel(
     with ExitStack() as ctx:
         ctx.enter_context(tc.manual_schedule())
         const = ctx.enter_context(tc.tile_pool(name="const", bufs=1))
-        raw_pool = ctx.enter_context(tc.tile_pool(name="raw", bufs=LOADS * PASSES))
+        raw_pool = ctx.enter_context(tc.tile_pool(name="raw", bufs=CHUNKS * PASSES))
         grouped_pool = ctx.enter_context(tc.tile_pool(name="grouped", bufs=CHUNKS))
         xq_pool = ctx.enter_context(tc.tile_pool(name="xq", bufs=CHUNKS))
         rows_pool = ctx.enter_context(tc.tile_pool(name="rows", bufs=UNITS))
@@ -74,12 +72,11 @@ def tile_gat_pa_kernel(
 
         x_raw = {}
 
-        def load_x(v):
+        def load_x(u):
             for g in range(PASSES):
-                raw = raw_pool.tile([P, PACK, LOAD], BF16, name="raw")
-                nc.sync.dma_start(out=raw[:], in_=x_rows[g, :, :, v * LOAD : (v + 1) * LOAD])
-                for u in range(v * LOAD // CHUNK, (v + 1) * LOAD // CHUNK):
-                    x_raw[(u, g)] = raw[:, :, u * CHUNK - v * LOAD : (u + 1) * CHUNK - v * LOAD]
+                raw = raw_pool.tile([P, PACK, CHUNK], BF16, name="raw")
+                nc.sync.dma_start(out=raw[:], in_=x_rows[g, :, :, u * CHUNK : (u + 1) * CHUNK])
+                x_raw[(u, g)] = raw
 
         def load_weight(h):
             words, scales, bias = weights[h]
@@ -96,8 +93,8 @@ def tile_gat_pa_kernel(
 
         load_x(0)
         load_weight(0)
-        for v in range(1, LOADS):
-            load_x(v)
+        for u in range(1, CHUNKS):
+            load_x(u)
         for h in range(1, HEADS):
             load_weight(h)
 
@@ -164,7 +161,7 @@ def tile_gat_pa_kernel(
             acc_of[k] = acc
 
         sum_sq_of = {}
-        excess_of = {}
+        raw_inverse_of = {}
 
         def add_bias(k):
             h = k // CHUNKS
@@ -185,15 +182,20 @@ def tile_gat_pa_kernel(
                 out=squares[:], in_=rows_of[k][:, i, :], func=ACT.Square, accum_out=sum_sq_of[k][:, i : i + 1]
             )
 
-        def clamp(k):
-            excess = small.tile([P, TILES], F32, name="excess")
-            nc.scalar.activation(out=excess[:], in_=sum_sq_of[k][:], func=ACT.Relu, bias=-EPS_SQUARED)
-            excess_of[k] = excess
-
         def invert(k):
+            raw = small.tile([P, TILES], F32, name="raw_inverse")
+            nc.scalar.activation(out=raw[:], in_=sum_sq_of[k][:], func=ACT.Abs_reciprocal_sqrt)
+            raw_inverse_of[k] = raw
+
+        def clamp(k):
             inverse = small.tile([P, TILES], F32, name="inverse")
-            nc.scalar.activation(
-                out=inverse[:], in_=excess_of[k][:], func=ACT.Abs_reciprocal_sqrt, bias=EPS_SQUARED
+            nc.gpsimd.tensor_scalar(
+                out=inverse[:],
+                in0=raw_inverse_of[k][:],
+                scalar1=1.0 / EPS,
+                scalar2=0.0,
+                op0=ALU.min,
+                op1=ALU.max,
             )
             inverse_of[k] = inverse
 
@@ -222,11 +224,10 @@ def tile_gat_pa_kernel(
             if k < UNITS:
                 sum_squares(k, 0)
             if 1 <= k <= UNITS:
+                invert(k - 1)
                 clamp(k - 1)
             if k < UNITS:
                 sum_squares(k, 1)
-            if 1 <= k <= UNITS:
-                invert(k - 1)
             if k + AHEAD < UNITS:
                 prepare(k + AHEAD)
             if k >= LAG:

@@ -26,7 +26,7 @@ UNITS = HEADS * CHUNKS
 QUADRANTS = 4
 RUN = 4
 EPS = 1e-12
-AHEAD = 2
+AHEAD = 3
 LAG = 3
 
 FLOPS = 2 * NODES * FEATURES * HEADS * HEAD_DIM
@@ -80,7 +80,7 @@ def tile_gat_pa_kernel(
 
         def load_weight(h):
             words, scales, bias = weights[h]
-            nc.sync.dma_start(out=bias_row[h][0:1, :], in_=bias.unsqueeze(0))
+            nc.gpsimd.dma_start(out=bias_row[h][0:1, :], in_=bias.unsqueeze(0))
             for q in range(QUADRANTS):
                 nc.sync.dma_start(
                     out=w_scales[h][32 * q : 32 * q + 4, :, :].bitcast(I32),
@@ -139,8 +139,8 @@ def tile_gat_pa_kernel(
 
         def prepare(k):
             h, u = divmod(k, CHUNKS)
-            if u == 0:
-                spread_bias(h)
+            if k < HEADS:
+                spread_bias(k)
             if h == 0:
                 quantise(u)
                 if u + 1 < CHUNKS:
@@ -210,10 +210,8 @@ def tile_gat_pa_kernel(
                     scalar2=None,
                     op0=ALU.mult,
                 )
-            nc.sync.dma_start(
-                out=out[h, u * CHUNK : (u + 1) * CHUNK, :].rearrange("(i p) d -> p i d", p=P),
-                in_=rows[:],
-            )
+                first = u * CHUNK + i * P
+                nc.sync.dma_start(out=out[h, first : first + P, :], in_=rows[:, i, :])
 
         regroup(0)
         for k in range(AHEAD):

@@ -26,7 +26,7 @@ UNITS = HEADS * CHUNKS
 QUADRANTS = 4
 RUN = 4
 EPS = 1e-12
-AHEAD = 3
+AHEAD = 2
 LAG = 3
 
 FLOPS = 2 * NODES * FEATURES * HEADS * HEAD_DIM
@@ -137,14 +137,8 @@ def tile_gat_pa_kernel(
         rows_of = {}
         inverse_of = {}
 
-        def prepare(k):
+        def multiply(k):
             h, u = divmod(k, CHUNKS)
-            if k < HEADS:
-                spread_bias(k)
-            if h == 0:
-                quantise(u)
-                if u + 1 < CHUNKS:
-                    regroup(u + 1)
             acc = psum.tile([P, TILES, HEAD_DIM], F32, name="acc")
             for i in range(TILES):
                 for g in range(PASSES):
@@ -213,7 +207,17 @@ def tile_gat_pa_kernel(
                 first = u * CHUNK + i * P
                 nc.sync.dma_start(out=out[h, first : first + P, :], in_=rows[:, i, :])
 
+        def prepare(k):
+            if k + 1 < CHUNKS:
+                regroup(k + 1)
+            if k < CHUNKS:
+                quantise(k)
+            if k % CHUNKS == CHUNKS - AHEAD and k // CHUNKS + 1 < HEADS:
+                spread_bias(k // CHUNKS + 1)
+            multiply(k)
+
         regroup(0)
+        spread_bias(0)
         for k in range(AHEAD):
             prepare(k)
         for k in range(UNITS + LAG):

@@ -111,15 +111,14 @@ def tile_gat_pa_kernel(
 
         def regroup(u):
             grouped = grouped_pool.tile([P, PASSES, CHUNK, PACK], BF16, name="grouped", align_bytes=64)
-            for g in range(PASSES):
-                nc.vector.tensor_copy(
-                    out=grouped[:, g, 0:P, :].rearrange("p (c i) t -> p c t i", i=RUN),
-                    in_=x_raw[(u, g)][:, :, 0:P].rearrange("p t (c i) -> p c t i", i=RUN),
-                )
-                nc.scalar.copy(
-                    out=grouped[:, g, P:CHUNK, :].rearrange("p (c i) t -> p c t i", i=RUN),
-                    in_=x_raw[(u, g)][:, :, P:CHUNK].rearrange("p t (c i) -> p c t i", i=RUN),
-                )
+            nc.vector.tensor_copy(
+                out=grouped[:, 0, :, :].rearrange("p (c i) t -> p c t i", i=RUN),
+                in_=x_raw[(u, 0)][:].rearrange("p t (c i) -> p c t i", i=RUN),
+            )
+            nc.scalar.copy(
+                out=grouped[:, 1, :, :].rearrange("p (c i) t -> p c t i", i=RUN),
+                in_=x_raw[(u, 1)][:].rearrange("p t (c i) -> p c t i", i=RUN),
+            )
             x_grouped[u] = grouped
 
         def quantise(u):

@@ -24,6 +24,7 @@ CHUNK = TILES * P
 CHUNKS = NODES // CHUNK
 UNITS = HEADS * CHUNKS
 QUADRANTS = 4
+WIDE = 512
 RUN = 4
 EPS = 1e-12
 AHEAD = 2
@@ -47,7 +48,8 @@ def tile_gat_pa_kernel(
         xq_pool = ctx.enter_context(tc.tile_pool(name="xq", bufs=CHUNKS))
         rows_pool = ctx.enter_context(tc.tile_pool(name="rows", bufs=UNITS))
         small = ctx.enter_context(tc.tile_pool(name="small", bufs=LAG + 3))
-        psum = ctx.enter_context(tc.psum_pool(name="psum", bufs=8))
+        psum = ctx.enter_context(tc.psum_pool(name="psum", bufs=7))
+        psum_idle = ctx.enter_context(tc.psum_pool(name="psum_idle", bufs=1))
 
         w_codes = []
         w_scales = []
@@ -65,6 +67,8 @@ def tile_gat_pa_kernel(
             w_scales.append(plane)
         ones = const.tile([P, P], BF16, name="ones")
         nc.vector.memset(ones[:], 1.0)
+        filler = const.tile([P, WIDE], BF16, name="filler")
+        nc.vector.memset(filler[:], 1.0)
         warm = const.tile([P, 1], F32, name="warm")
         nc.vector.memset(warm[:], 1.0)
 
@@ -214,6 +218,16 @@ def tile_gat_pa_kernel(
             if k % CHUNKS == CHUNKS - AHEAD and k // CHUNKS + 1 < HEADS:
                 spread_bias(k // CHUNKS + 1)
             multiply(k)
+
+        idle_bank = psum_idle.tile([P, WIDE], F32, name="idle_bank")
+        for repeat in range(4):
+            nc.tensor.matmul(out=idle_bank[:], lhsT=ones[:], rhs=filler[:], start=True, stop=True)
+        for g in range(PASSES):
+            flat = x_raw[(0, g)][:].rearrange("p t n -> p (t n)")
+            for half in range(2):
+                nc.tensor.matmul(
+                    out=idle_bank[:], lhsT=ones[:], rhs=flat[:, half * WIDE : (half + 1) * WIDE], start=True, stop=True
+                )
 
         regroup(0)
         spread_bias(0)

@@ -24,10 +24,11 @@ CHUNK = TILES * P
 CHUNKS = NODES // CHUNK
 UNITS = HEADS * CHUNKS
 QUADRANTS = 4
-WIDE = 512
 RUN = 4
 EPS = 1e-12
-AHEAD = 2
+REGROUP_VECTOR = {2: 2, 4: 3}
+REGROUP_SCALAR = {1: 2, 4: 3}
+QUANTISE = {1: 1, 3: 2, 6: 3}
 LAG = 3
 
 FLOPS = 2 * NODES * FEATURES * HEADS * HEAD_DIM
@@ -48,31 +49,24 @@ def tile_gat_pa_kernel(
         xq_pool = ctx.enter_context(tc.tile_pool(name="xq", bufs=CHUNKS))
         rows_pool = ctx.enter_context(tc.tile_pool(name="rows", bufs=UNITS))
         small = ctx.enter_context(tc.tile_pool(name="small", bufs=LAG + 3))
-        psum = ctx.enter_context(tc.psum_pool(name="psum", bufs=7))
-        psum_idle = ctx.enter_context(tc.psum_pool(name="psum_idle", bufs=1))
+        psum = ctx.enter_context(tc.psum_pool(name="psum", bufs=8))
 
-        w_codes = []
-        w_scales = []
-        bias_row = []
-        bias_all = {}
-        for h in range(HEADS):
-            row = const.tile([P, HEAD_DIM], BF16, name="bias_row%d" % h)
-            nc.vector.memset(row[:], 0.0)
-            bias_row.append(row)
-        for h in range(HEADS):
-            codes = const.tile([P, PASSES, HEAD_DIM], U32, name="w_codes%d" % h, align_bytes=64)
-            plane = const.tile([P, PASSES, HEAD_DIM], U8, name="w_scales%d" % h, align_bytes=64)
-            nc.vector.memset(plane[:].bitcast(I32), 0)
-            w_codes.append(codes)
-            w_scales.append(plane)
-        ones = const.tile([P, P], BF16, name="ones")
-        nc.vector.memset(ones[:], 1.0)
-        filler = const.tile([P, WIDE], BF16, name="filler")
-        nc.vector.memset(filler[:], 1.0)
+        bias_row = const.tile([P, HEADS, HEAD_DIM], BF16, name="bias_row")
+        nc.vector.memset(bias_row[:].rearrange("p h d -> p (h d)").bitcast(I32), 0)
         warm = const.tile([P, 1], F32, name="warm")
         nc.vector.memset(warm[:], 1.0)
+        ones = const.tile([P, P], BF16, name="ones")
+        nc.vector.memset(ones[:], 1.0)
+        w_scales = const.tile([P, HEADS, PASSES, HEAD_DIM], U8, name="w_scales", align_bytes=64)
+        nc.vector.memset(w_scales[:].rearrange("p h g n -> p (h g n)").bitcast(I32), 0)
+        w_codes = []
+        for h in range(HEADS):
+            codes = const.tile([P, PASSES, HEAD_DIM], U32, name="w_codes%d" % h, align_bytes=64)
+            w_codes.append(codes)
 
         nc.scalar.activation(out=warm[:], in_=warm[:], func=ACT.Abs_reciprocal_sqrt)
+        for h in range(HEADS):
+            nc.gpsimd.dma_start(out=bias_row[0:1, h, :], in_=weights[h][2].unsqueeze(0))
 
         x_raw = {}
 
@@ -84,46 +78,57 @@ def tile_gat_pa_kernel(
 
         def load_weight(h):
             words, scales, bias = weights[h]
-            nc.gpsimd.dma_start(out=bias_row[h][0:1, :], in_=bias.unsqueeze(0))
-            for q in range(QUADRANTS):
-                nc.sync.dma_start(
-                    out=w_scales[h][32 * q : 32 * q + 4, :, :].bitcast(I32),
-                    in_=scales[:, 4 * q : 4 * q + 4, :].rearrange("g r n -> r g n").bitcast(I32),
-                )
             nc.sync.dma_start(
                 out=w_codes[h][:].bitcast(I32),
                 in_=words.rearrange("g p n t -> p g (n t)").bitcast(I32),
             )
+            for q in range(QUADRANTS):
+                nc.sync.dma_start(
+                    out=w_scales[32 * q : 32 * q + 4, h, :, :].bitcast(I32),
+                    in_=scales[:, 4 * q : 4 * q + 4, :].rearrange("g r n -> r g n").bitcast(I32),
+                )
 
         load_x(0)
         load_weight(0)
-        for u in range(1, CHUNKS):
+        load_x(1)
+        load_weight(1)
+        load_weight(2)
+        for u in range(2, CHUNKS):
             load_x(u)
-        for h in range(1, HEADS):
-            load_weight(h)
+
+        bias_all = const.tile([P, HEADS, HEAD_DIM], F32, name="bias_all")
 
         def spread_bias(h):
             bank = psum.tile([P, TILES, HEAD_DIM], F32, name="acc")
-            nc.tensor.matmul(out=bank[:, 0, :], lhsT=ones[:], rhs=bias_row[h][:], start=True, stop=True)
-            spread = const.tile([P, HEAD_DIM], F32, name="bias_all%d" % h)
-            nc.scalar.copy(out=spread[:], in_=bank[:, 0, :])
-            bias_all[h] = spread
+            nc.tensor.matmul(out=bank[:, 0, :], lhsT=ones[:], rhs=bias_row[:, h, :], start=True, stop=True)
+            nc.vector.tensor_copy(out=bias_all[:, h, :], in_=bank[:, 0, :])
 
         x_grouped = {}
         x_codes = {}
         x_scales = {}
 
-        def regroup(u):
+        def open_grouped(u):
+            if u not in x_grouped:
+                x_grouped[u] = new_grouped()
+            return x_grouped[u]
+
+        def new_grouped():
             grouped = grouped_pool.tile([P, PASSES, CHUNK, PACK], BF16, name="grouped", align_bytes=64)
+            return grouped
+
+        def regroup_vector(u):
+            grouped = open_grouped(u)
             nc.vector.tensor_copy(
                 out=grouped[:, 0, :, :].rearrange("p (c i) t -> p c t i", i=RUN),
                 in_=x_raw[(u, 0)][:].rearrange("p t (c i) -> p c t i", i=RUN),
             )
+
+        def regroup_scalar(u, first=0):
+            grouped = open_grouped(u)
             nc.scalar.copy(
-                out=grouped[:, 1, :, :].rearrange("p (c i) t -> p c t i", i=RUN),
-                in_=x_raw[(u, 1)][:].rearrange("p t (c i) -> p c t i", i=RUN),
+                out=grouped[:, 1, first:CHUNK, :].rearrange("p (c i) t -> p c t i", i=RUN),
+                in_=x_raw[(u, 1)][:, :, first:CHUNK].rearrange("p t (c i) -> p c t i", i=RUN),
             )
-            x_grouped[u] = grouped
 
         def quantise(u):
             codes = xq_pool.tile([P, PASSES * CHUNK], U32, name="x_codes", align_bytes=64)
@@ -141,7 +146,7 @@ def tile_gat_pa_kernel(
         inverse_of = {}
 
         def multiply(k):
-            h, u = divmod(k, CHUNKS)
+            u, h = divmod(k, HEADS)
             acc = psum.tile([P, TILES, HEAD_DIM], F32, name="acc")
             for i in range(TILES):
                 for g in range(PASSES):
@@ -151,7 +156,7 @@ def tile_gat_pa_kernel(
                         lhsT=x_codes[u][:, nodes].bitcast(FP8X4),
                         lhsT_scale=x_scales[u][:, nodes],
                         rhs=w_codes[h][:, g, :].bitcast(FP8X4),
-                        rhs_scale=w_scales[h][:, g, :],
+                        rhs_scale=w_scales[:, h, g, :],
                         start=(g == 0),
                         stop=(g == PASSES - 1),
                     )
@@ -161,12 +166,12 @@ def tile_gat_pa_kernel(
         raw_inverse_of = {}
 
         def add_bias(k):
-            h = k // CHUNKS
+            h = k % HEADS
             rows = rows_pool.tile([P, TILES, HEAD_DIM], F32, name="rows")
             nc.vector.tensor_tensor(
                 out=rows[:],
                 in0=acc_of[k][:],
-                in1=bias_all[h][:].unsqueeze(1).to_broadcast([P, TILES, HEAD_DIM]),
+                in1=bias_all[:, h, :].unsqueeze(1).to_broadcast([P, TILES, HEAD_DIM]),
                 op=ALU.add,
             )
             rows_of[k] = rows
@@ -197,7 +202,7 @@ def tile_gat_pa_kernel(
             inverse_of[k] = inverse
 
         def scale_and_store(k):
-            h, u = divmod(k, CHUNKS)
+            u, h = divmod(k, HEADS)
             rows = rows_of[k]
             for i in range(TILES):
                 nc.vector.tensor_scalar(
@@ -210,40 +215,37 @@ def tile_gat_pa_kernel(
                 first = u * CHUNK + i * P
                 nc.sync.dma_start(out=out[h, first : first + P, :], in_=rows[:, i, :])
 
-        def prepare(k):
-            if k + 1 < CHUNKS:
-                regroup(k + 1)
-            if k < CHUNKS:
-                quantise(k)
-            if k % CHUNKS == CHUNKS - AHEAD and k // CHUNKS + 1 < HEADS:
-                spread_bias(k // CHUNKS + 1)
-            multiply(k)
-
-        idle_bank = psum_idle.tile([P, WIDE], F32, name="idle_bank")
-        for repeat in range(4):
-            nc.tensor.matmul(out=idle_bank[:], lhsT=ones[:], rhs=filler[:], start=True, stop=True)
-        for g in range(PASSES):
-            flat = x_raw[(0, g)][:].rearrange("p t n -> p (t n)")
-            for half in range(2):
-                nc.tensor.matmul(
-                    out=idle_bank[:], lhsT=ones[:], rhs=flat[:, half * WIDE : (half + 1) * WIDE], start=True, stop=True
-                )
-
-        regroup(0)
+        regroup_vector(0)
+        nc.vector.tensor_copy(
+            out=x_grouped[0][:, 1, 0:P, :].rearrange("p (c i) t -> p c t i", i=RUN),
+            in_=x_raw[(0, 1)][:, :, 0:P].rearrange("p t (c i) -> p c t i", i=RUN),
+        )
+        regroup_scalar(0, P)
+        quantise(0)
         spread_bias(0)
-        for k in range(AHEAD):
-            prepare(k)
+        multiply(0)
+        regroup_vector(1)
+        regroup_scalar(1)
         for k in range(UNITS + LAG):
             if k < UNITS:
                 add_bias(k)
-            if k < UNITS:
+                if k + 1 < HEADS:
+                    spread_bias(k + 1)
+                    multiply(k + 1)
                 sum_squares(k, 0)
             if 1 <= k <= UNITS:
                 invert(k - 1)
                 clamp(k - 1)
             if k < UNITS:
                 sum_squares(k, 1)
-            if k + AHEAD < UNITS:
-                prepare(k + AHEAD)
             if k >= LAG:
                 scale_and_store(k - LAG)
+            if k in REGROUP_SCALAR:
+                regroup_scalar(REGROUP_SCALAR[k])
+            if k in REGROUP_VECTOR:
+                regroup_vector(REGROUP_VECTOR[k])
+            if k in QUANTISE:
+                u = QUANTISE[k]
+                quantise(u)
+                for h in range(HEADS):
+                    multiply(u * HEADS + h)

@@ -24,11 +24,13 @@ CHUNK = TILES * P
 CHUNKS = NODES // CHUNK
 UNITS = HEADS * CHUNKS
 QUADRANTS = 4
+HALVES = 2
+HALF = NODES // HALVES
+PER_HALF = HALF // CHUNK
+WIDE = 512
 RUN = 4
 EPS = 1e-12
-REGROUP_VECTOR = {2: 2, 4: 3}
-REGROUP_SCALAR = {1: 2, 4: 3}
-QUANTISE = {1: 1, 3: 2, 6: 3}
+ORDER = [(u, h) for h in range(HEADS) for u in range(2)] + [(u, h) for u in range(2, CHUNKS) for h in range(HEADS)]
 LAG = 3
 
 FLOPS = 2 * NODES * FEATURES * HEADS * HEAD_DIM
@@ -44,12 +46,13 @@ def tile_gat_pa_kernel(
     with ExitStack() as ctx:
         ctx.enter_context(tc.manual_schedule())
         const = ctx.enter_context(tc.tile_pool(name="const", bufs=1))
-        raw_pool = ctx.enter_context(tc.tile_pool(name="raw", bufs=CHUNKS * PASSES))
+        raw_pool = ctx.enter_context(tc.tile_pool(name="raw", bufs=HALVES * PASSES))
         grouped_pool = ctx.enter_context(tc.tile_pool(name="grouped", bufs=CHUNKS))
         xq_pool = ctx.enter_context(tc.tile_pool(name="xq", bufs=CHUNKS))
         rows_pool = ctx.enter_context(tc.tile_pool(name="rows", bufs=UNITS))
         small = ctx.enter_context(tc.tile_pool(name="small", bufs=LAG + 3))
-        psum = ctx.enter_context(tc.psum_pool(name="psum", bufs=8))
+        psum = ctx.enter_context(tc.psum_pool(name="psum", bufs=7))
+        psum_idle = ctx.enter_context(tc.psum_pool(name="psum_idle", bufs=1))
 
         bias_row = const.tile([P, HEADS, HEAD_DIM], BF16, name="bias_row")
         nc.vector.memset(bias_row[:].rearrange("p h d -> p (h d)").bitcast(I32), 0)
@@ -64,17 +67,18 @@ def tile_gat_pa_kernel(
             codes = const.tile([P, PASSES, HEAD_DIM], U32, name="w_codes%d" % h, align_bytes=64)
             w_codes.append(codes)
 
-        nc.scalar.activation(out=warm[:], in_=warm[:], func=ACT.Abs_reciprocal_sqrt)
         for h in range(HEADS):
             nc.gpsimd.dma_start(out=bias_row[0:1, h, :], in_=weights[h][2].unsqueeze(0))
 
+        nc.scalar.activation(out=warm[:], in_=warm[:], func=ACT.Abs_reciprocal_sqrt)
+
         x_raw = {}
 
-        def load_x(u):
+        def load_x(half):
             for g in range(PASSES):
-                raw = raw_pool.tile([P, PACK, CHUNK], BF16, name="raw")
-                nc.sync.dma_start(out=raw[:], in_=x_rows[g, :, :, u * CHUNK : (u + 1) * CHUNK])
-                x_raw[(u, g)] = raw
+                raw = raw_pool.tile([P, PACK, HALF], BF16, name="raw")
+                nc.sync.dma_start(out=raw[:], in_=x_rows[g, :, :, half * HALF : (half + 1) * HALF])
+                x_raw[(half, g)] = raw
 
         def load_weight(h):
             words, scales, bias = weights[h]
@@ -90,18 +94,19 @@ def tile_gat_pa_kernel(
 
         load_x(0)
         load_weight(0)
-        load_x(1)
         load_weight(1)
+        load_x(1)
         load_weight(2)
-        for u in range(2, CHUNKS):
-            load_x(u)
 
         bias_all = const.tile([P, HEADS, HEAD_DIM], F32, name="bias_all")
 
-        def spread_bias(h):
+        def spread_biases(first, last):
             bank = psum.tile([P, TILES, HEAD_DIM], F32, name="acc")
-            nc.tensor.matmul(out=bank[:, 0, :], lhsT=ones[:], rhs=bias_row[:, h, :], start=True, stop=True)
-            nc.vector.tensor_copy(out=bias_all[:, h, :], in_=bank[:, 0, :])
+            heads = slice(first, last)
+            nc.tensor.matmul(
+                out=bank[:, 0 : last - first, :], lhsT=ones[:], rhs=bias_row[:, heads, :], start=True, stop=True
+            )
+            nc.scalar.copy(out=bias_all[:, heads, :], in_=bank[:, 0 : last - first, :])
 
         x_grouped = {}
         x_codes = {}
@@ -116,18 +121,11 @@ def tile_gat_pa_kernel(
             grouped = grouped_pool.tile([P, PASSES, CHUNK, PACK], BF16, name="grouped", align_bytes=64)
             return grouped
 
-        def regroup_vector(u):
-            grouped = open_grouped(u)
-            nc.vector.tensor_copy(
-                out=grouped[:, 0, :, :].rearrange("p (c i) t -> p c t i", i=RUN),
-                in_=x_raw[(u, 0)][:].rearrange("p t (c i) -> p c t i", i=RUN),
-            )
-
-        def regroup_scalar(u, first=0):
-            grouped = open_grouped(u)
-            nc.scalar.copy(
-                out=grouped[:, 1, first:CHUNK, :].rearrange("p (c i) t -> p c t i", i=RUN),
-                in_=x_raw[(u, 1)][:, :, first:CHUNK].rearrange("p t (c i) -> p c t i", i=RUN),
+        def regroup(engine_copy, u, g):
+            half, c = divmod(u, PER_HALF)
+            engine_copy(
+                out=open_grouped(u)[:, g, :, :].rearrange("p (c i) t -> p c t i", i=RUN),
+                in_=x_raw[(half, g)][:, :, c * CHUNK : (c + 1) * CHUNK].rearrange("p t (c i) -> p c t i", i=RUN),
             )
 
         def quantise(u):
@@ -146,7 +144,7 @@ def tile_gat_pa_kernel(
         inverse_of = {}
 
         def multiply(k):
-            u, h = divmod(k, HEADS)
+            u, h = ORDER[k]
             acc = psum.tile([P, TILES, HEAD_DIM], F32, name="acc")
             for i in range(TILES):
                 for g in range(PASSES):
@@ -166,7 +164,7 @@ def tile_gat_pa_kernel(
         raw_inverse_of = {}
 
         def add_bias(k):
-            h = k % HEADS
+            h = ORDER[k][1]
             rows = rows_pool.tile([P, TILES, HEAD_DIM], F32, name="rows")
             nc.vector.tensor_tensor(
                 out=rows[:],
@@ -202,7 +200,7 @@ def tile_gat_pa_kernel(
             inverse_of[k] = inverse
 
         def scale_and_store(k):
-            u, h = divmod(k, HEADS)
+            u, h = ORDER[k]
             rows = rows_of[k]
             for i in range(TILES):
                 nc.vector.tensor_scalar(
@@ -215,23 +213,22 @@ def tile_gat_pa_kernel(
                 first = u * CHUNK + i * P
                 nc.sync.dma_start(out=out[h, first : first + P, :], in_=rows[:, i, :])
 
-        regroup_vector(0)
-        nc.vector.tensor_copy(
-            out=x_grouped[0][:, 1, 0:P, :].rearrange("p (c i) t -> p c t i", i=RUN),
-            in_=x_raw[(0, 1)][:, :, 0:P].rearrange("p t (c i) -> p c t i", i=RUN),
-        )
-        regroup_scalar(0, P)
+        idle_bank = psum_idle.tile([P, WIDE], F32, name="idle_bank")
+        for t in range(PACK):
+            nc.tensor.matmul(out=idle_bank[:], lhsT=ones[:], rhs=x_raw[(0, 0)][:, t, :], start=True, stop=True)
+
+        regroup(nc.vector.tensor_copy, 0, 0)
+        regroup(nc.vector.tensor_copy, 1, 0)
+        regroup(nc.vector.tensor_copy, 0, 1)
+        regroup(nc.scalar.copy, 1, 1)
+        spread_biases(0, 2)
         quantise(0)
-        spread_bias(0)
-        multiply(0)
-        regroup_vector(1)
-        regroup_scalar(1)
+        quantise(1)
+        for k in range(4):
+            multiply(k)
         for k in range(UNITS + LAG):
             if k < UNITS:
                 add_bias(k)
-                if k + 1 < HEADS:
-                    spread_bias(k + 1)
-                    multiply(k + 1)
                 sum_squares(k, 0)
             if 1 <= k <= UNITS:
                 invert(k - 1)
@@ -240,12 +237,19 @@ def tile_gat_pa_kernel(
                 sum_squares(k, 1)
             if k >= LAG:
                 scale_and_store(k - LAG)
-            if k in REGROUP_SCALAR:
-                regroup_scalar(REGROUP_SCALAR[k])
-            if k in REGROUP_VECTOR:
-                regroup_vector(REGROUP_VECTOR[k])
-            if k in QUANTISE:
-                u = QUANTISE[k]
-                quantise(u)
-                for h in range(HEADS):
-                    multiply(u * HEADS + h)
+            if k == 0:
+                spread_biases(2, 3)
+            if k == 1:
+                regroup(nc.vector.tensor_copy, 2, 0)
+                regroup(nc.vector.tensor_copy, 3, 0)
+                regroup(nc.scalar.copy, 2, 1)
+            if k == 2:
+                regroup(nc.scalar.copy, 3, 1)
+            if k == 3:
+                quantise(2)
+                for j in range(4, 9):
+                    multiply(j)
+            if k == 4:
+                quantise(3)
+                for j in range(9, UNITS):
+                    multiply(j)

@@ -30,8 +30,10 @@ PER_HALF = HALF // CHUNK
 WIDE = 512
 RUN = 4
 EPS = 1e-12
-ORDER = [(u, h) for h in range(HEADS) for u in range(2)] + [(u, h) for u in range(2, CHUNKS) for h in range(HEADS)]
-LAG = 3
+ORDER = [(PER_HALF * half + c, h) for half in range(HALVES) for h in range(HEADS - 1) for c in range(PER_HALF)] + [
+    (u, HEADS - 1) for u in range(CHUNKS)
+]
+LAG = 2
 
 FLOPS = 2 * NODES * FEATURES * HEADS * HEAD_DIM
 
@@ -94,8 +96,8 @@ def tile_gat_pa_kernel(
 
         load_x(0)
         load_weight(0)
-        load_weight(1)
         load_x(1)
+        load_weight(1)
         load_weight(2)
 
         bias_all = const.tile([P, HEADS, HEAD_DIM], F32, name="bias_all")
@@ -106,7 +108,7 @@ def tile_gat_pa_kernel(
             nc.tensor.matmul(
                 out=bank[:, 0 : last - first, :], lhsT=ones[:], rhs=bias_row[:, heads, :], start=True, stop=True
             )
-            nc.scalar.copy(out=bias_all[:, heads, :], in_=bank[:, 0 : last - first, :])
+            return lambda: nc.scalar.copy(out=bias_all[:, heads, :], in_=bank[:, 0 : last - first, :])
 
         x_grouped = {}
         x_codes = {}
@@ -218,38 +220,41 @@ def tile_gat_pa_kernel(
             nc.tensor.matmul(out=idle_bank[:], lhsT=ones[:], rhs=x_raw[(0, 0)][:, t, :], start=True, stop=True)
 
         regroup(nc.vector.tensor_copy, 0, 0)
-        regroup(nc.vector.tensor_copy, 1, 0)
         regroup(nc.vector.tensor_copy, 0, 1)
+        regroup(nc.scalar.copy, 1, 0)
         regroup(nc.scalar.copy, 1, 1)
-        spread_biases(0, 2)
+        copy_biases_01 = spread_biases(0, 2)
+        copy_bias_2 = spread_biases(2, 3)
+        copy_biases_01()
         quantise(0)
         quantise(1)
         for k in range(4):
             multiply(k)
-        for k in range(UNITS + LAG):
-            if k < UNITS:
-                add_bias(k)
-                sum_squares(k, 0)
-            if 1 <= k <= UNITS:
-                invert(k - 1)
-                clamp(k - 1)
-            if k < UNITS:
-                sum_squares(k, 1)
-            if k >= LAG:
-                scale_and_store(k - LAG)
+        for k in range(UNITS):
+            add_bias(k)
             if k == 0:
-                spread_biases(2, 3)
-            if k == 1:
-                regroup(nc.vector.tensor_copy, 2, 0)
                 regroup(nc.vector.tensor_copy, 3, 0)
+                regroup(nc.scalar.copy, 2, 0)
+            if k == 1:
+                regroup(nc.vector.tensor_copy, 3, 1)
+            sum_squares(k, 0)
+            if k == 0:
                 regroup(nc.scalar.copy, 2, 1)
-            if k == 2:
-                regroup(nc.scalar.copy, 3, 1)
-            if k == 3:
+            sum_squares(k, 1)
+            invert(k)
+            clamp(k)
+            if k == 1:
+                copy_bias_2()
+                quantise(3)
                 quantise(2)
                 for j in range(4, 9):
                     multiply(j)
+            if k == 3:
+                scale_and_store(0)
+            if k >= 3:
+                scale_and_store(k - LAG)
             if k == 4:
-                quantise(3)
                 for j in range(9, UNITS):
                     multiply(j)
+        for k in range(UNITS - LAG, UNITS):
+            scale_and_store(k)

@@ -70,7 +70,7 @@ def tile_gat_pa_kernel(
             w_codes.append(codes)
 
         for h in range(HEADS):
-            nc.gpsimd.dma_start(out=bias_row[0:1, h, :], in_=weights[h][2].unsqueeze(0))
+            nc.scalar.dma_start(out=bias_row[0:1, h, :], in_=weights[h][2].unsqueeze(0))
 
         nc.scalar.activation(out=warm[:], in_=warm[:], func=ACT.Abs_reciprocal_sqrt)
 

@@ -30,10 +30,8 @@ PER_HALF = HALF // CHUNK
 WIDE = 512
 RUN = 4
 EPS = 1e-12
-ORDER = [(PER_HALF * half + c, h) for half in range(HALVES) for h in range(HEADS - 1) for c in range(PER_HALF)] + [
-    (u, HEADS - 1) for u in range(CHUNKS)
-]
-LAG = 2
+ORDER = [(PER_HALF * half + c, h) for half in range(HALVES) for h in range(HEADS) for c in range(PER_HALF)]
+LAG = 3
 
 FLOPS = 2 * NODES * FEATURES * HEADS * HEAD_DIM
 
@@ -53,11 +51,13 @@ def tile_gat_pa_kernel(
         xq_pool = ctx.enter_context(tc.tile_pool(name="xq", bufs=CHUNKS))
         rows_pool = ctx.enter_context(tc.tile_pool(name="rows", bufs=UNITS))
         small = ctx.enter_context(tc.tile_pool(name="small", bufs=LAG + 3))
-        psum = ctx.enter_context(tc.psum_pool(name="psum", bufs=7))
-        psum_idle = ctx.enter_context(tc.psum_pool(name="psum_idle", bufs=1))
+        psum = ctx.enter_context(tc.psum_pool(name="psum", bufs=8))
 
         bias_row = const.tile([P, HEADS, HEAD_DIM], BF16, name="bias_row")
-        nc.vector.memset(bias_row[:].rearrange("p h d -> p (h d)").bitcast(I32), 0)
+        for h in range(HEADS):
+            nc.sync.dma_start(out=bias_row[P - 1 : P, h, :], in_=weights[h][2].unsqueeze(0))
+        for first, last in ((0, P - 32), (P - 32, P - 1)):
+            nc.vector.memset(bias_row[first:last, :, :].rearrange("p h d -> p (h d)").bitcast(I32), 0)
         warm = const.tile([P, 1], F32, name="warm")
         nc.vector.memset(warm[:], 1.0)
         ones = const.tile([P, P], BF16, name="ones")
@@ -68,9 +68,6 @@ def tile_gat_pa_kernel(
         for h in range(HEADS):
             codes = const.tile([P, PASSES, HEAD_DIM], U32, name="w_codes%d" % h, align_bytes=64)
             w_codes.append(codes)
-
-        for h in range(HEADS):
-            nc.scalar.dma_start(out=bias_row[0:1, h, :], in_=weights[h][2].unsqueeze(0))
 
         nc.scalar.activation(out=warm[:], in_=warm[:], func=ACT.Abs_reciprocal_sqrt)
 
@@ -215,46 +212,46 @@ def tile_gat_pa_kernel(
                 first = u * CHUNK + i * P
                 nc.sync.dma_start(out=out[h, first : first + P, :], in_=rows[:, i, :])
 
-        idle_bank = psum_idle.tile([P, WIDE], F32, name="idle_bank")
-        for t in range(PACK):
-            nc.tensor.matmul(out=idle_bank[:], lhsT=ones[:], rhs=x_raw[(0, 0)][:, t, :], start=True, stop=True)
-
-        regroup(nc.vector.tensor_copy, 0, 0)
-        regroup(nc.vector.tensor_copy, 0, 1)
-        regroup(nc.scalar.copy, 1, 0)
-        regroup(nc.scalar.copy, 1, 1)
         copy_biases_01 = spread_biases(0, 2)
         copy_bias_2 = spread_biases(2, 3)
         copy_biases_01()
-        quantise(0)
-        quantise(1)
-        for k in range(4):
+        copy_bias_2()
+        idle_bank = psum.tile([P, TILES, HEAD_DIM], F32, name="acc")
+        for t in range(PACK):
+            nc.tensor.matmul(
+                out=idle_bank[:],
+                lhsT=ones[:],
+                rhs=x_raw[(0, 0)][:, t, :].rearrange("p (i d) -> p i d", i=TILES),
+                start=True,
+                stop=True,
+            )
+
+        for g in range(PASSES):
+            regroup(nc.vector.tensor_copy, 0, g)
+            regroup(nc.scalar.copy, 1, g)
+        for u in range(PER_HALF):
+            quantise(u)
+        for k in range(HEADS * PER_HALF):
             multiply(k)
-        for k in range(UNITS):
-            add_bias(k)
+        for k in range(UNITS + LAG):
+            if k < UNITS:
+                add_bias(k)
             if k == 0:
-                regroup(nc.vector.tensor_copy, 3, 0)
-                regroup(nc.scalar.copy, 2, 0)
-            if k == 1:
-                regroup(nc.vector.tensor_copy, 3, 1)
-            sum_squares(k, 0)
-            if k == 0:
-                regroup(nc.scalar.copy, 2, 1)
-            sum_squares(k, 1)
-            invert(k)
-            clamp(k)
-            if k == 1:
-                copy_bias_2()
-                quantise(3)
-                quantise(2)
-                for j in range(4, 9):
-                    multiply(j)
-            if k == 3:
-                scale_and_store(0)
-            if k >= 3:
+                for g in range(PASSES):
+                    regroup(nc.vector.tensor_copy, 3, g)
+                    regroup(nc.scalar.copy, 2, g)
+            if k < UNITS:
+                sum_squares(k, 0)
+            if 1 <= k <= UNITS:
+                invert(k - 1)
+                clamp(k - 1)
+            if k < UNITS:
+                sum_squares(k, 1)
+            if k >= LAG:
                 scale_and_store(k - LAG)
-            if k == 4:
-                for j in range(9, UNITS):
+            if k == 1:
+                quantise(3)
+            if k == 3:
+                quantise(2)
+                for j in range(HEADS * PER_HALF, UNITS):
                     multiply(j)
-        for k in range(UNITS - LAG, UNITS):
-            scale_and_store(k)

@@ -54,8 +54,6 @@ def tile_gat_pa_kernel(
         psum = ctx.enter_context(tc.psum_pool(name="psum", bufs=8))
 
         bias_row = const.tile([P, HEADS, HEAD_DIM], BF16, name="bias_row")
-        for h in range(HEADS):
-            nc.sync.dma_start(out=bias_row[P - 1 : P, h, :], in_=weights[h][2].unsqueeze(0))
         for first, last in ((0, P - 32), (P - 32, P - 1)):
             nc.vector.memset(bias_row[first:last, :, :].rearrange("p h d -> p (h d)").bitcast(I32), 0)
         warm = const.tile([P, 1], F32, name="warm")
@@ -78,6 +76,9 @@ def tile_gat_pa_kernel(
                 raw = raw_pool.tile([P, PACK, HALF], BF16, name="raw")
                 nc.sync.dma_start(out=raw[:], in_=x_rows[g, :, :, half * HALF : (half + 1) * HALF])
                 x_raw[(half, g)] = raw
+                if half == 0 and g == 0:
+                    for h in range(HEADS):
+                        nc.sync.dma_start(out=bias_row[P - 1 : P, h, :], in_=weights[h][2].unsqueeze(0))
 
         def load_weight(h):
             words, scales, bias = weights[h]
@@ -127,14 +128,19 @@ def tile_gat_pa_kernel(
                 in_=x_raw[(half, g)][:, :, c * CHUNK : (c + 1) * CHUNK].rearrange("p t (c i) -> p c t i", i=RUN),
             )
 
-        def quantise(u):
+        def quantise(u, first, last):
+            if u not in x_codes:
+                open_codes(u)
+            nodes = slice(first * CHUNK, last * CHUNK)
+            nc.vector.quantize_mx(
+                out=x_codes[u][:, nodes].bitcast(FP8X4),
+                scales=x_scales[u][:, nodes],
+                in_=x_grouped[u][:, first:last, :, :].rearrange("p g n t -> p (g n t)"),
+            )
+
+        def open_codes(u):
             codes = xq_pool.tile([P, PASSES * CHUNK], U32, name="x_codes", align_bytes=64)
             plane = xq_pool.tile([P, PASSES * CHUNK], U8, name="x_scales", align_bytes=64)
-            nc.vector.quantize_mx(
-                out=codes[:].bitcast(FP8X4),
-                scales=plane[:],
-                in_=x_grouped[u][:].rearrange("p g n t -> p (g n t)"),
-            )
             x_codes[u] = codes
             x_scales[u] = plane
 
@@ -162,15 +168,20 @@ def tile_gat_pa_kernel(
         sum_sq_of = {}
         raw_inverse_of = {}
 
-        def add_bias(k):
+        def add_bias(k, tiles=slice(0, TILES)):
             h = ORDER[k][1]
-            rows = rows_pool.tile([P, TILES, HEAD_DIM], F32, name="rows")
+            if k not in rows_of:
+                open_rows(k)
+            width = tiles.stop - tiles.start
             nc.vector.tensor_tensor(
-                out=rows[:],
-                in0=acc_of[k][:],
-                in1=bias_all[:, h, :].unsqueeze(1).to_broadcast([P, TILES, HEAD_DIM]),
+                out=rows_of[k][:, tiles, :],
+                in0=acc_of[k][:, tiles, :],
+                in1=bias_all[:, h, :].unsqueeze(1).to_broadcast([P, width, HEAD_DIM]),
                 op=ALU.add,
             )
+
+        def open_rows(k):
+            rows = rows_pool.tile([P, TILES, HEAD_DIM], F32, name="rows")
             rows_of[k] = rows
             sum_sq = small.tile([P, TILES], F32, name="sum_sq")
             sum_sq_of[k] = sum_sq
@@ -186,9 +197,9 @@ def tile_gat_pa_kernel(
             nc.scalar.activation(out=raw[:], in_=sum_sq_of[k][:], func=ACT.Abs_reciprocal_sqrt)
             raw_inverse_of[k] = raw
 
-        def clamp(k):
+        def clamp(k, engine_tensor_scalar):
             inverse = small.tile([P, TILES], F32, name="inverse")
-            nc.gpsimd.tensor_scalar(
+            engine_tensor_scalar(
                 out=inverse[:],
                 in0=raw_inverse_of[k][:],
                 scalar1=1.0 / EPS,
@@ -198,26 +209,23 @@ def tile_gat_pa_kernel(
             )
             inverse_of[k] = inverse
 
-        def scale_and_store(k):
+        def scale_and_store(k, i):
             u, h = ORDER[k]
             rows = rows_of[k]
-            for i in range(TILES):
-                nc.vector.tensor_scalar(
-                    out=rows[:, i, :],
-                    in0=rows[:, i, :],
-                    scalar1=inverse_of[k][:, i : i + 1],
-                    scalar2=None,
-                    op0=ALU.mult,
-                )
-                first = u * CHUNK + i * P
-                nc.sync.dma_start(out=out[h, first : first + P, :], in_=rows[:, i, :])
+            nc.vector.tensor_scalar(
+                out=rows[:, i, :],
+                in0=rows[:, i, :],
+                scalar1=inverse_of[k][:, i : i + 1],
+                scalar2=None,
+                op0=ALU.mult,
+            )
+            first = u * CHUNK + i * P
+            nc.sync.dma_start(out=out[h, first : first + P, :], in_=rows[:, i, :])
 
         copy_biases_01 = spread_biases(0, 2)
         copy_bias_2 = spread_biases(2, 3)
-        copy_biases_01()
-        copy_bias_2()
         idle_bank = psum.tile([P, TILES, HEAD_DIM], F32, name="acc")
-        for t in range(PACK):
+        for t in range(PACK - 1):
             nc.tensor.matmul(
                 out=idle_bank[:],
                 lhsT=ones[:],
@@ -229,29 +237,49 @@ def tile_gat_pa_kernel(
         for g in range(PASSES):
             regroup(nc.vector.tensor_copy, 0, g)
             regroup(nc.scalar.copy, 1, g)
+            if g == 0:
+                copy_biases_01()
+                copy_bias_2()
         for u in range(PER_HALF):
-            quantise(u)
+            for g in range(PASSES):
+                quantise(u, g, g + 1)
         for k in range(HEADS * PER_HALF):
             multiply(k)
-        for k in range(UNITS + LAG):
-            if k < UNITS:
-                add_bias(k)
+        last = UNITS - 1
+        for k in range(last):
+            add_bias(k)
             if k == 0:
                 for g in range(PASSES):
                     regroup(nc.vector.tensor_copy, 3, g)
                     regroup(nc.scalar.copy, 2, g)
-            if k < UNITS:
-                sum_squares(k, 0)
-            if 1 <= k <= UNITS:
+            sum_squares(k, 0)
+            if k >= 1:
                 invert(k - 1)
-                clamp(k - 1)
-            if k < UNITS:
-                sum_squares(k, 1)
+                clamp(k - 1, nc.gpsimd.tensor_scalar)
+            sum_squares(k, 1)
             if k >= LAG:
-                scale_and_store(k - LAG)
+                for i in range(TILES):
+                    scale_and_store(k - LAG, i)
             if k == 1:
-                quantise(3)
+                quantise(3, 0, PASSES)
             if k == 3:
-                quantise(2)
+                quantise(2, 0, PASSES)
                 for j in range(HEADS * PER_HALF, UNITS):
                     multiply(j)
+
+        for i in range(TILES):
+            add_bias(last, slice(i, i + 1))
+        sum_squares(last, 0)
+        invert(last - 1)
+        sum_squares(last, 1)
+        invert(last)
+        for i in range(TILES):
+            scale_and_store(last - 3, i)
+        scale_and_store(last - 2, 0)
+        clamp(last - 1, nc.vector.tensor_scalar)
+        scale_and_store(last - 2, 1)
+        scale_and_store(last - 1, 0)
+        clamp(last, nc.vector.tensor_scalar)
+        scale_and_store(last - 1, 1)
+        for i in range(TILES):
+            scale_and_store(last, i)

@@ -67,6 +67,9 @@ def tile_gat_pa_kernel(
             codes = const.tile([P, PASSES, HEAD_DIM], U32, name="w_codes%d" % h, align_bytes=64)
             w_codes.append(codes)
 
+        for h in range(1, HEADS):
+            nc.gpsimd.dma_start(out=bias_row[P - 1 : P, h, :], in_=weights[h][2].unsqueeze(0))
+
         nc.scalar.activation(out=warm[:], in_=warm[:], func=ACT.Abs_reciprocal_sqrt)
 
         x_raw = {}
@@ -77,8 +80,7 @@ def tile_gat_pa_kernel(
                 nc.sync.dma_start(out=raw[:], in_=x_rows[g, :, :, half * HALF : (half + 1) * HALF])
                 x_raw[(half, g)] = raw
                 if half == 0 and g == 0:
-                    for h in range(HEADS):
-                        nc.sync.dma_start(out=bias_row[P - 1 : P, h, :], in_=weights[h][2].unsqueeze(0))
+                    nc.sync.dma_start(out=bias_row[P - 1 : P, 0, :], in_=weights[0][2].unsqueeze(0))
 
         def load_weight(h):
             words, scales, bias = weights[h]
@@ -100,13 +102,15 @@ def tile_gat_pa_kernel(
 
         bias_all = const.tile([P, HEADS, HEAD_DIM], F32, name="bias_all")
 
-        def spread_biases(first, last):
+        bias_bank = {}
+
+        def spread_bias(h):
             bank = psum.tile([P, TILES, HEAD_DIM], F32, name="acc")
-            heads = slice(first, last)
-            nc.tensor.matmul(
-                out=bank[:, 0 : last - first, :], lhsT=ones[:], rhs=bias_row[:, heads, :], start=True, stop=True
-            )
-            return lambda: nc.scalar.copy(out=bias_all[:, heads, :], in_=bank[:, 0 : last - first, :])
+            nc.tensor.matmul(out=bank[:, 0, :], lhsT=ones[:], rhs=bias_row[:, h, :], start=True, stop=True)
+            bias_bank[h] = bank
+
+        def copy_bias(h):
+            nc.scalar.copy(out=bias_all[:, h, :], in_=bias_bank[h][:, 0, :])
 
         x_grouped = {}
         x_codes = {}
@@ -222,8 +226,6 @@ def tile_gat_pa_kernel(
             first = u * CHUNK + i * P
             nc.sync.dma_start(out=out[h, first : first + P, :], in_=rows[:, i, :])
 
-        copy_biases_01 = spread_biases(0, 2)
-        copy_bias_2 = spread_biases(2, 3)
         idle_bank = psum.tile([P, TILES, HEAD_DIM], F32, name="acc")
         for t in range(PACK - 1):
             nc.tensor.matmul(
@@ -234,17 +236,20 @@ def tile_gat_pa_kernel(
                 stop=True,
             )
 
+        spread_bias(0)
+
         for g in range(PASSES):
             regroup(nc.vector.tensor_copy, 0, g)
             regroup(nc.scalar.copy, 1, g)
-            if g == 0:
-                copy_biases_01()
-                copy_bias_2()
+        copy_bias(0)
         for u in range(PER_HALF):
             for g in range(PASSES):
                 quantise(u, g, g + 1)
-        for k in range(HEADS * PER_HALF):
-            multiply(k)
+        for h in range(HEADS):
+            for c in range(PER_HALF):
+                multiply(PER_HALF * h + c)
+            if h + 1 < HEADS:
+                spread_bias(h + 1)
         last = UNITS - 1
         for k in range(last):
             add_bias(k)
@@ -252,6 +257,7 @@ def tile_gat_pa_kernel(
                 for g in range(PASSES):
                     regroup(nc.vector.tensor_copy, 3, g)
                     regroup(nc.scalar.copy, 2, g)
+                copy_bias(1)
             sum_squares(k, 0)
             if k >= 1:
                 invert(k - 1)
@@ -261,6 +267,7 @@ def tile_gat_pa_kernel(
                 for i in range(TILES):
                     scale_and_store(k - LAG, i)
             if k == 1:
+                copy_bias(2)
                 quantise(3, 0, PASSES)
             if k == 3:
                 quantise(2, 0, PASSES)

from contextlib import ExitStack

import concourse.mybir as mybir

F32 = mybir.dt.float32
BF16 = mybir.dt.bfloat16
I32 = mybir.dt.int32
U32 = mybir.dt.uint32
U8 = mybir.dt.uint8
FP8X4 = mybir.dt.float8_e4m3fn_x4
ACT = mybir.ActivationFunctionType
ALU = mybir.AluOpType

P = 128
PACK = 4
K_PASS = P * PACK
FEATURES = 1024
NODES = 1024
HEADS = 3
HEAD_DIM = 256
PASSES = FEATURES // K_PASS
TILES = 2
CHUNK = TILES * P
CHUNKS = NODES // CHUNK
UNITS = HEADS * CHUNKS
QUADRANTS = 4
HALVES = 2
HALF = NODES // HALVES
PER_HALF = HALF // CHUNK
WIDE = 512
RUN = 4
EPS = 1e-12
ORDER = [(PER_HALF * half + c, h) for half in range(HALVES) for h in range(HEADS) for c in range(PER_HALF)]
LAG = 3

FLOPS = 2 * NODES * FEATURES * HEADS * HEAD_DIM


def tile_gat_pa_kernel(
    tc, x, W1_words, W1_scales, b1, W2_words, W2_scales, b2, W3_words, W3_scales, b3, out
):
    nc = tc.nc
    weights = ((W1_words, W1_scales, b1), (W2_words, W2_scales, b2), (W3_words, W3_scales, b3))
    x_rows = x.rearrange("b f i j -> (b f) (i j)").rearrange("(g p t) n -> g p t n", p=P, t=PACK)

    with ExitStack() as ctx:
        ctx.enter_context(tc.manual_schedule())
        const = ctx.enter_context(tc.tile_pool(name="const", bufs=1))
        raw_pool = ctx.enter_context(tc.tile_pool(name="raw", bufs=HALVES * PASSES))
        grouped_pool = ctx.enter_context(tc.tile_pool(name="grouped", bufs=CHUNKS))
        xq_pool = ctx.enter_context(tc.tile_pool(name="xq", bufs=CHUNKS))
        rows_pool = ctx.enter_context(tc.tile_pool(name="rows", bufs=UNITS))
        small = ctx.enter_context(tc.tile_pool(name="small", bufs=LAG + 3))
        psum = ctx.enter_context(tc.psum_pool(name="psum", bufs=8))

        bias_row = const.tile([P, HEADS, HEAD_DIM], BF16, name="bias_row")
        for first, last in ((0, P - 32), (P - 32, P - 1)):
            nc.vector.memset(bias_row[first:last, :, :].rearrange("p h d -> p (h d)").bitcast(I32), 0)
        warm = const.tile([P, 1], F32, name="warm")
        nc.vector.memset(warm[:], 1.0)
        ones = const.tile([P, P], BF16, name="ones")
        nc.vector.memset(ones[:], 1.0)
        w_scales = const.tile([P, HEADS, PASSES, HEAD_DIM], U8, name="w_scales", align_bytes=64)
        nc.vector.memset(w_scales[:].rearrange("p h g n -> p (h g n)").bitcast(I32), 0)
        w_codes = []
        for h in range(HEADS):
            codes = const.tile([P, PASSES, HEAD_DIM], U32, name="w_codes%d" % h, align_bytes=64)
            w_codes.append(codes)

        for h in range(1, HEADS):
            nc.gpsimd.dma_start(out=bias_row[P - 1 : P, h, :], in_=weights[h][2].unsqueeze(0))

        nc.scalar.activation(out=warm[:], in_=warm[:], func=ACT.Abs_reciprocal_sqrt)

        x_raw = {}

        def load_x(half):
            for g in range(PASSES):
                raw = raw_pool.tile([P, PACK, HALF], BF16, name="raw")
                nc.sync.dma_start(out=raw[:], in_=x_rows[g, :, :, half * HALF : (half + 1) * HALF])
                x_raw[(half, g)] = raw
                if half == 0 and g == 0:
                    nc.sync.dma_start(out=bias_row[P - 1 : P, 0, :], in_=weights[0][2].unsqueeze(0))

        def load_weight(h):
            words, scales, bias = weights[h]
            nc.sync.dma_start(
                out=w_codes[h][:].bitcast(I32),
                in_=words.rearrange("g p n t -> p g (n t)").bitcast(I32),
            )
            for q in range(QUADRANTS):
                nc.sync.dma_start(
                    out=w_scales[32 * q : 32 * q + 4, h, :, :].bitcast(I32),
                    in_=scales[:, 4 * q : 4 * q + 4, :].rearrange("g r n -> r g n").bitcast(I32),
                )

        load_x(0)
        load_weight(0)
        load_x(1)
        load_weight(1)
        load_weight(2)

        bias_all = const.tile([P, HEADS, HEAD_DIM], F32, name="bias_all")

        bias_bank = {}

        def spread_bias(h):
            bank = psum.tile([P, TILES, HEAD_DIM], F32, name="acc")
            nc.tensor.matmul(out=bank[:, 0, :], lhsT=ones[:], rhs=bias_row[:, h, :], start=True, stop=True)
            bias_bank[h] = bank

        def copy_bias(h):
            nc.scalar.copy(out=bias_all[:, h, :], in_=bias_bank[h][:, 0, :])

        x_grouped = {}
        x_codes = {}
        x_scales = {}

        def open_grouped(u):
            if u not in x_grouped:
                x_grouped[u] = new_grouped()
            return x_grouped[u]

        def new_grouped():
            grouped = grouped_pool.tile([P, PASSES, CHUNK, PACK], BF16, name="grouped", align_bytes=64)
            return grouped

        def regroup(engine_copy, u, g):
            half, c = divmod(u, PER_HALF)
            engine_copy(
                out=open_grouped(u)[:, g, :, :].rearrange("p (c i) t -> p c t i", i=RUN),
                in_=x_raw[(half, g)][:, :, c * CHUNK : (c + 1) * CHUNK].rearrange("p t (c i) -> p c t i", i=RUN),
            )

        def quantise(u, first, last):
            if u not in x_codes:
                open_codes(u)
            nodes = slice(first * CHUNK, last * CHUNK)
            nc.vector.quantize_mx(
                out=x_codes[u][:, nodes].bitcast(FP8X4),
                scales=x_scales[u][:, nodes],
                in_=x_grouped[u][:, first:last, :, :].rearrange("p g n t -> p (g n t)"),
            )

        def open_codes(u):
            codes = xq_pool.tile([P, PASSES * CHUNK], U32, name="x_codes", align_bytes=64)
            plane = xq_pool.tile([P, PASSES * CHUNK], U8, name="x_scales", align_bytes=64)
            x_codes[u] = codes
            x_scales[u] = plane

        acc_of = {}
        rows_of = {}
        inverse_of = {}

        def multiply(k):
            u, h = ORDER[k]
            acc = psum.tile([P, TILES, HEAD_DIM], F32, name="acc")
            for i in range(TILES):
                for g in range(PASSES):
                    nodes = slice(g * CHUNK + i * P, g * CHUNK + (i + 1) * P)
                    nc.tensor.matmul_mx(
                        out=acc[:, i, :],
                        lhsT=x_codes[u][:, nodes].bitcast(FP8X4),
                        lhsT_scale=x_scales[u][:, nodes],
                        rhs=w_codes[h][:, g, :].bitcast(FP8X4),
                        rhs_scale=w_scales[:, h, g, :],
                        start=(g == 0),
                        stop=(g == PASSES - 1),
                    )
            acc_of[k] = acc

        sum_sq_of = {}
        raw_inverse_of = {}

        def add_bias(k, tiles=slice(0, TILES)):
            h = ORDER[k][1]
            if k not in rows_of:
                open_rows(k)
            width = tiles.stop - tiles.start
            nc.vector.tensor_tensor(
                out=rows_of[k][:, tiles, :],
                in0=acc_of[k][:, tiles, :],
                in1=bias_all[:, h, :].unsqueeze(1).to_broadcast([P, width, HEAD_DIM]),
                op=ALU.add,
            )

        def open_rows(k):
            rows = rows_pool.tile([P, TILES, HEAD_DIM], F32, name="rows")
            rows_of[k] = rows
            sum_sq = small.tile([P, TILES], F32, name="sum_sq")
            sum_sq_of[k] = sum_sq

        def sum_squares(k, i):
            squares = small.tile([P, HEAD_DIM], F32, name="squares")
            nc.scalar.activation(
                out=squares[:], in_=rows_of[k][:, i, :], func=ACT.Square, accum_out=sum_sq_of[k][:, i : i + 1]
            )

        def invert(k):
            raw = small.tile([P, TILES], F32, name="raw_inverse")
            nc.scalar.activation(out=raw[:], in_=sum_sq_of[k][:], func=ACT.Abs_reciprocal_sqrt)
            raw_inverse_of[k] = raw

        def clamp(k, engine_tensor_scalar):
            inverse = small.tile([P, TILES], F32, name="inverse")
            engine_tensor_scalar(
                out=inverse[:],
                in0=raw_inverse_of[k][:],
                scalar1=1.0 / EPS,
                scalar2=0.0,
                op0=ALU.min,
                op1=ALU.max,
            )
            inverse_of[k] = inverse

        def scale_and_store(k, i):
            u, h = ORDER[k]
            rows = rows_of[k]
            nc.vector.tensor_scalar(
                out=rows[:, i, :],
                in0=rows[:, i, :],
                scalar1=inverse_of[k][:, i : i + 1],
                scalar2=None,
                op0=ALU.mult,
            )
            first = u * CHUNK + i * P
            nc.sync.dma_start(out=out[h, first : first + P, :], in_=rows[:, i, :])

        idle_bank = psum.tile([P, TILES, HEAD_DIM], F32, name="acc")
        for t in range(PACK - 1):
            nc.tensor.matmul(
                out=idle_bank[:],
                lhsT=ones[:],
                rhs=x_raw[(0, 0)][:, t, :].rearrange("p (i d) -> p i d", i=TILES),
                start=True,
                stop=True,
            )

        spread_bias(0)

        for g in range(PASSES):
            regroup(nc.vector.tensor_copy, 0, g)
            regroup(nc.scalar.copy, 1, g)
        copy_bias(0)
        for u in range(PER_HALF):
            for g in range(PASSES):
                quantise(u, g, g + 1)
        for h in range(HEADS):
            for c in range(PER_HALF):
                multiply(PER_HALF * h + c)
            if h + 1 < HEADS:
                spread_bias(h + 1)
        last = UNITS - 1
        for k in range(last):
            add_bias(k)
            if k == 0:
                for g in range(PASSES):
                    regroup(nc.vector.tensor_copy, 3, g)
                    regroup(nc.scalar.copy, 2, g)
                copy_bias(1)
            sum_squares(k, 0)
            if k >= 1:
                invert(k - 1)
                clamp(k - 1, nc.gpsimd.tensor_scalar)
            sum_squares(k, 1)
            if k >= LAG:
                for i in range(TILES):
                    scale_and_store(k - LAG, i)
            if k == 1:
                copy_bias(2)
                quantise(3, 0, PASSES)
            if k == 3:
                quantise(2, 0, PASSES)
                for j in range(HEADS * PER_HALF, UNITS):
                    multiply(j)

        for i in range(TILES):
            add_bias(last, slice(i, i + 1))
        sum_squares(last, 0)
        invert(last - 1)
        sum_squares(last, 1)
        invert(last)
        for i in range(TILES):
            scale_and_store(last - 3, i)
        scale_and_store(last - 2, 0)
        clamp(last - 1, nc.vector.tensor_scalar)
        scale_and_store(last - 2, 1)
        scale_and_store(last - 1, 0)
        clamp(last, nc.vector.tensor_scalar)
        scale_and_store(last - 1, 1)
        for i in range(TILES):
            scale_and_store(last, i)
